import numpy as np
import ml_dtypes


def mxq(x, axis, fmt="e4m3"):
    dtype, down = {"e4m3": (ml_dtypes.float8_e4m3fn, 7), "e5m2": (ml_dtypes.float8_e5m2, 14)}[fmt]
    v = np.moveaxis(np.asarray(x, np.float32).astype(ml_dtypes.bfloat16).astype(np.float64), axis, -1)
    blocks = v.reshape(v.shape[:-1] + (-1, 32))
    amax = np.abs(blocks).max(-1, keepdims=True)
    byte = np.maximum(np.where(amax > 0, np.frexp(amax)[1] - 1 + 127, 0) - down, 1)
    scale = np.exp2(byte - 127.0)
    codes = (blocks / scale).astype(np.float32).astype(dtype).astype(np.float64)
    return np.moveaxis((codes * scale).reshape(v.shape), -1, axis)


WIDE = False


def mx_kscale(k):
    if not WIDE:
        return np.ones(k)
    levels = np.array([10, -10, 5, -5, 0])
    a = np.random.permutation(np.resize(levels, k // 512 * 4)).reshape(k // 512, 4)
    idx = np.arange(k)
    return np.exp2(a[idx // 512, idx % 128 // 32])


BF16 = ml_dtypes.bfloat16


def bf(x):
    return np.asarray(x, np.float32).astype(BF16)


def f64(x):
    return np.asarray(x).astype(np.float64)


B, T, E, Q = 4, 4096, 128, 512
N = B * T


def setup_inputs():
    s = mx_kscale(Q)
    return {"y": bf(np.random.standard_normal((B, T, Q)) * s),
            "w_swiglu": bf(np.random.standard_normal((2 * E, Q)) / np.sqrt(Q) / s)}


def reference(y, w_swiglu):
    uv = mxq(f64(y).reshape(N, Q), 1, "e4m3") @ mxq(f64(w_swiglu).T, 0, "e4m3")
    u, v = uv[:, :E], uv[:, E:]
    ao = mxq(u.T, 1, "e4m3") @ mxq(v, 0, "e4m3")
    return ao / B * E ** (-0.5)

@@ -1,0 +1,203 @@
+from contextlib import ExitStack
+
+import concourse.mybir as mybir
+from concourse.masks import make_identity
+
+F32 = mybir.dt.float32
+BF16 = mybir.dt.bfloat16
+U32 = mybir.dt.uint32
+U8 = mybir.dt.uint8
+FP8X4 = mybir.dt.float8_e4m3fn_x4
+
+P = 128
+PACK = 4
+TOKENS = 4 * 4096
+FEATURES = 512
+E = 128
+GROUP = P * PACK
+GROUPS = TOKENS // GROUP
+PAIRS = GROUPS // 2
+WORDS = FEATURES // 2
+SCALE = 1.0 / 4.0 / (128.0 ** 0.5)
+
+FLOPS = 2 * TOKENS * FEATURES * 2 * E + 2 * TOKENS * E * E
+
+VECTOR_TURNS = (2, 5, 9)
+TURNS = 10
+DEPTH = 4
+
+
+def tile_retentionmechanism_pa_t_kernel(tc, y, w_swiglu, out):
+    nc = tc.nc
+    with ExitStack() as ctx:
+        ctx.enter_context(tc.manual_schedule())
+        keep = ctx.enter_context(tc.tile_pool(name="keep", bufs=1))
+        ring = ctx.enter_context(tc.tile_pool(name="ring", bufs=1))
+        psum = ctx.enter_context(tc.psum_pool(name="psum", bufs=1))
+
+        y_rows = y.flatten_outer_dims().rearrange("(g p j) q -> g p j q", p=P, j=PACK)
+
+        y_sb = []
+        for g in range(GROUPS):
+            y_sb.append(keep.tile([P, PACK, FEATURES], BF16, name="y%d" % g))
+        w_sb = keep.tile([P, 2, FEATURES], BF16, name="w_sb")
+        nc.sync.dma_start(out=y_sb[0][:, 0:2, :], in_=y_rows[0][:, 0:2, :])
+        nc.scalar.dma_start(out=w_sb[:], in_=w_swiglu.rearrange("(a p) q -> p a q", p=P))
+        nc.sync.dma_start(out=y_sb[0][:, 2:4, :], in_=y_rows[0][:, 2:4, :])
+        for g in range(1, GROUPS):
+            nc.sync.dma_start(out=y_sb[g][:], in_=y_rows[g])
+
+        ident = keep.tile([P, P], F32, name="ident")
+        make_identity(nc, ident[:])
+
+        w_codes = keep.tile([P, 2 * E], U32, name="w_codes", align_bytes=64)
+        w_scales = keep.tile([P, 2 * E], U8, name="w_scales", align_bytes=64)
+        uv_codes = keep.tile([P, GROUPS, 2 * E], U32, name="uv_codes", align_bytes=64)
+        uv_scales = keep.tile([P, GROUPS, 2 * E], U8, name="uv_scales", align_bytes=64)
+
+        state = {"turn": 0}
+
+        def drain(dst, src):
+            turn = state["turn"]
+            state["turn"] = turn + 1
+            if turn % TURNS in VECTOR_TURNS:
+                nc.vector.tensor_copy(out=dst, in_=src)
+            else:
+                nc.scalar.copy(out=dst, in_=src)
+
+        def transpose_two(rows_a, rows_b, bank):
+            xt = psum.tile([P, 2, 2, P], F32, name="xt", tag="bank%d" % bank)
+            for a, rows in enumerate((rows_a, rows_b)):
+                words = rows.bitcast(F32)
+                for u in range(2):
+                    nc.tensor.transpose(xt[:, a, u, :], words[:, u * P:(u + 1) * P], ident[:])
+            return xt
+
+        xts = {}
+        ygs = {}
+        ycs = {}
+        uvs = {}
+        ugs = {}
+
+        def transposes(g):
+            for h in range(2):
+                xts[(g, h)] = transpose_two(
+                    y_sb[g][:, 2 * h, :], y_sb[g][:, 2 * h + 1, :], (2 * g + h) % 4
+                )
+
+        def drain_y(g, h):
+            if h == 0:
+                ygs[g] = ring.tile(
+                    [P, PACK, P, PACK], BF16, name="yg", tag="yg%d" % (g % DEPTH), align_bytes=64
+                )
+            dst = ygs[g][:].bitcast(F32)[:, 2 * h:2 * h + 2, :, :]
+            drain(dst, xts[(g, h)][:].rearrange("p a u n -> p a n u"))
+
+        def quant_y(g):
+            codes = ring.tile([P, GROUP], U32, name="yc", tag="yc%d" % (g % DEPTH), align_bytes=64)
+            scales = ring.tile([P, GROUP], U8, name="ys", tag="ys%d" % (g % DEPTH), align_bytes=64)
+            nc.vector.quantize_mx(
+                out=codes[:].bitcast(FP8X4),
+                scales=scales[:],
+                in_=ygs[g][:].rearrange("p j n t -> p (j n t)"),
+            )
+            ycs[g] = (codes, scales)
+
+        def mm1(g):
+            codes, scales = ycs[g]
+            for h in range(2):
+                bank = psum.tile([P, PACK, E], F32, name="uv", tag="bank%d" % (4 + (2 * g + h) % 4))
+                for j in range(PACK):
+                    nc.tensor.matmul_mx(
+                        out=bank[:, j, :],
+                        lhsT=codes[:, j * P:(j + 1) * P].bitcast(FP8X4),
+                        lhsT_scale=scales[:, j * P:(j + 1) * P],
+                        rhs=w_codes[:, h * E:(h + 1) * E].bitcast(FP8X4),
+                        rhs_scale=w_scales[:, h * E:(h + 1) * E],
+                        start=True,
+                        stop=True,
+                    )
+                uvs[(g, h)] = bank
+
+        def drain_uv(g, h):
+            if h == 0:
+                ugs[g] = ring.tile(
+                    [P, 2, E, PACK], BF16, name="ug", tag="ug%d" % (g % DEPTH), align_bytes=64
+                )
+            drain(ugs[g][:, h, :, :], uvs[(g, h)][:].rearrange("p j d -> p d j"))
+
+        def quant_uv(g):
+            nc.vector.quantize_mx(
+                out=uv_codes[:, g, :].bitcast(FP8X4),
+                scales=uv_scales[:, g, :],
+                in_=ugs[g][:].rearrange("p h d j -> p (h d j)"),
+            )
+
+        acc = []
+
+        def mm2(g):
+            if g == 0:
+                acc.append(psum.tile([P, E], F32, name="acc", tag="bank0"))
+            nc.tensor.matmul_mx(
+                out=acc[0][:],
+                lhsT=uv_codes[:, g, 0:E].bitcast(FP8X4),
+                lhsT_scale=uv_scales[:, g, 0:E],
+                rhs=uv_codes[:, g, E:2 * E].bitcast(FP8X4),
+                rhs_scale=uv_scales[:, g, E:2 * E],
+                start=(g == 0),
+                stop=(g == GROUPS - 1),
+            )
+
+        def prepare_w():
+            wt = transpose_two(w_sb[:, 0, :], w_sb[:, 1, :], 4)
+            wg = keep.tile([P, 2, E, PACK], BF16, name="wg", align_bytes=64)
+            nc.vector.tensor_copy(
+                out=wg[:].bitcast(F32), in_=wt[:].rearrange("p a u n -> p a n u")
+            )
+            nc.vector.quantize_mx(
+                out=w_codes[:].bitcast(FP8X4),
+                scales=w_scales[:],
+                in_=wg[:].rearrange("p a n t -> p (a n t)"),
+            )
+
+        for s in range(PAIRS + 2):
+            a = 2 * s
+            b = a + 1
+            if s < PAIRS:
+                transposes(a)
+                if s == 0:
+                    prepare_w()
+                transposes(b)
+            if 1 <= s <= PAIRS:
+                mm1(a - 2)
+                mm1(b - 2)
+            if s < PAIRS:
+                drain_y(a, 0)
+                drain_y(a, 1)
+            if s == PAIRS - 1:
+                for g in range(16):
+                    mm2(g)
+            if s >= 2:
+                quant_uv(b - 4)
+            if s < PAIRS:
+                drain_y(b, 0)
+                drain_y(b, 1)
+                quant_y(a)
+            if 1 <= s <= PAIRS:
+                drain_uv(a - 2, 0)
+                drain_uv(a - 2, 1)
+            if s < PAIRS:
+                quant_y(b)
+            if 1 <= s <= PAIRS:
+                drain_uv(b - 2, 0)
+                drain_uv(b - 2, 1)
+                quant_uv(a - 2)
+            if s == PAIRS:
+                for g in range(16, GROUPS - 2):
+                    mm2(g)
+        mm2(GROUPS - 2)
+        mm2(GROUPS - 1)
+
+        res = keep.tile([P, E], F32, name="res")
+        nc.scalar.mul(res[:], acc[0][:], SCALE)
+        nc.sync.dma_start(out=out, in_=res[:])

@@ -22,8 +22,8 @@ SCALE = 1.0 / 4.0 / (128.0 ** 0.5)
 
 FLOPS = 2 * TOKENS * FEATURES * 2 * E + 2 * TOKENS * E * E
 
-VECTOR_TURNS = (2, 5, 9)
-TURNS = 10
+VECTOR_TURNS = (3,)
+TURNS = 4
 DEPTH = 4
 
 

@@ -22,8 +22,6 @@ SCALE = 1.0 / 4.0 / (128.0 ** 0.5)
 
 FLOPS = 2 * TOKENS * FEATURES * 2 * E + 2 * TOKENS * E * E
 
-VECTOR_TURNS = (3,)
-TURNS = 4
 DEPTH = 4
 
 
@@ -55,12 +53,8 @@ def tile_retentionmechanism_pa_t_kernel(tc, y, w_swiglu, out):
         uv_codes = keep.tile([P, GROUPS, 2 * E], U32, name="uv_codes", align_bytes=64)
         uv_scales = keep.tile([P, GROUPS, 2 * E], U8, name="uv_scales", align_bytes=64)
 
-        state = {"turn": 0}
-
-        def drain(dst, src):
-            turn = state["turn"]
-            state["turn"] = turn + 1
-            if turn % TURNS in VECTOR_TURNS:
+        def drain(dst, src, on_vector):
+            if on_vector:
                 nc.vector.tensor_copy(out=dst, in_=src)
             else:
                 nc.scalar.copy(out=dst, in_=src)
@@ -91,7 +85,7 @@ def tile_retentionmechanism_pa_t_kernel(tc, y, w_swiglu, out):
                     [P, PACK, P, PACK], BF16, name="yg", tag="yg%d" % (g % DEPTH), align_bytes=64
                 )
             dst = ygs[g][:].bitcast(F32)[:, 2 * h:2 * h + 2, :, :]
-            drain(dst, xts[(g, h)][:].rearrange("p a u n -> p a n u"))
+            drain(dst, xts[(g, h)][:].rearrange("p a u n -> p a n u"), h == 1 and g % 2 == 1)
 
         def quant_y(g):
             codes = ring.tile([P, GROUP], U32, name="yc", tag="yc%d" % (g % DEPTH), align_bytes=64)
@@ -124,7 +118,7 @@ def tile_retentionmechanism_pa_t_kernel(tc, y, w_swiglu, out):
                 ugs[g] = ring.tile(
                     [P, 2, E, PACK], BF16, name="ug", tag="ug%d" % (g % DEPTH), align_bytes=64
                 )
-            drain(ugs[g][:, h, :, :], uvs[(g, h)][:].rearrange("p j d -> p d j"))
+            drain(ugs[g][:, h, :, :], uvs[(g, h)][:].rearrange("p j d -> p d j"), h == 1 and (g % 2 == 1 or g % 8 == 4))
 
         def quant_uv(g):
             nc.vector.quantize_mx(

@@ -16,13 +16,15 @@ FEATURES = 512
 E = 128
 GROUP = P * PACK
 GROUPS = TOKENS // GROUP
-PAIRS = GROUPS // 2
 WORDS = FEATURES // 2
 SCALE = 1.0 / 4.0 / (128.0 ** 0.5)
 
 FLOPS = 2 * TOKENS * FEATURES * 2 * E + 2 * TOKENS * E * E
 
-DEPTH = 4
+BANKS = 8
+FIRST_RUN = 2
+RUN = 3
+DEPTH = 6
 
 
 def tile_retentionmechanism_pa_t_kernel(tc, y, w_swiglu, out):
@@ -53,14 +55,21 @@ def tile_retentionmechanism_pa_t_kernel(tc, y, w_swiglu, out):
         uv_codes = keep.tile([P, GROUPS, 2 * E], U32, name="uv_codes", align_bytes=64)
         uv_scales = keep.tile([P, GROUPS, 2 * E], U8, name="uv_scales", align_bytes=64)
 
+        state = {"fills": 0}
+
+        def next_bank():
+            fills = state["fills"]
+            state["fills"] = fills + 1
+            return "bank%d" % (fills % BANKS)
+
         def drain(dst, src, on_vector):
             if on_vector:
                 nc.vector.tensor_copy(out=dst, in_=src)
             else:
                 nc.scalar.copy(out=dst, in_=src)
 
-        def transpose_two(rows_a, rows_b, bank):
-            xt = psum.tile([P, 2, 2, P], F32, name="xt", tag="bank%d" % bank)
+        def transpose_two(rows_a, rows_b):
+            xt = psum.tile([P, 2, 2, P], F32, name="xt", tag=next_bank())
             for a, rows in enumerate((rows_a, rows_b)):
                 words = rows.bitcast(F32)
                 for u in range(2):
@@ -75,9 +84,7 @@ def tile_retentionmechanism_pa_t_kernel(tc, y, w_swiglu, out):
 
         def transposes(g):
             for h in range(2):
-                xts[(g, h)] = transpose_two(
-                    y_sb[g][:, 2 * h, :], y_sb[g][:, 2 * h + 1, :], (2 * g + h) % 4
-                )
+                xts[(g, h)] = transpose_two(y_sb[g][:, 2 * h, :], y_sb[g][:, 2 * h + 1, :])
 
         def drain_y(g, h):
             if h == 0:
@@ -85,7 +92,7 @@ def tile_retentionmechanism_pa_t_kernel(tc, y, w_swiglu, out):
                     [P, PACK, P, PACK], BF16, name="yg", tag="yg%d" % (g % DEPTH), align_bytes=64
                 )
             dst = ygs[g][:].bitcast(F32)[:, 2 * h:2 * h + 2, :, :]
-            drain(dst, xts[(g, h)][:].rearrange("p a u n -> p a n u"), h == 1 and g % 2 == 1)
+            drain(dst, xts[(g, h)][:].rearrange("p a u n -> p a n u"), (2 * g + h) % 4 == 3)
 
         def quant_y(g):
             codes = ring.tile([P, GROUP], U32, name="yc", tag="yc%d" % (g % DEPTH), align_bytes=64)
@@ -100,7 +107,7 @@ def tile_retentionmechanism_pa_t_kernel(tc, y, w_swiglu, out):
         def mm1(g):
             codes, scales = ycs[g]
             for h in range(2):
-                bank = psum.tile([P, PACK, E], F32, name="uv", tag="bank%d" % (4 + (2 * g + h) % 4))
+                bank = psum.tile([P, PACK, E], F32, name="uv", tag=next_bank())
                 for j in range(PACK):
                     nc.tensor.matmul_mx(
                         out=bank[:, j, :],
@@ -118,7 +125,11 @@ def tile_retentionmechanism_pa_t_kernel(tc, y, w_swiglu, out):
                 ugs[g] = ring.tile(
                     [P, 2, E, PACK], BF16, name="ug", tag="ug%d" % (g % DEPTH), align_bytes=64
                 )
-            drain(ugs[g][:, h, :, :], uvs[(g, h)][:].rearrange("p j d -> p d j"), h == 1 and (g % 2 == 1 or g % 8 == 4))
+            drain(
+                ugs[g][:, h, :, :],
+                uvs[(g, h)][:].rearrange("p j d -> p d j"),
+                (2 * g + h) % 16 in range(3, 16, 3),
+            )
 
         def quant_uv(g):
             nc.vector.quantize_mx(
@@ -131,7 +142,7 @@ def tile_retentionmechanism_pa_t_kernel(tc, y, w_swiglu, out):
 
         def mm2(g):
             if g == 0:
-                acc.append(psum.tile([P, E], F32, name="acc", tag="bank0"))
+                acc.append(psum.tile([P, E], F32, name="acc", tag=next_bank()))
             nc.tensor.matmul_mx(
                 out=acc[0][:],
                 lhsT=uv_codes[:, g, 0:E].bitcast(FP8X4),
@@ -143,7 +154,7 @@ def tile_retentionmechanism_pa_t_kernel(tc, y, w_swiglu, out):
             )
 
         def prepare_w():
-            wt = transpose_two(w_sb[:, 0, :], w_sb[:, 1, :], 4)
+            wt = transpose_two(w_sb[:, 0, :], w_sb[:, 1, :])
             wg = keep.tile([P, 2, E, PACK], BF16, name="wg", align_bytes=64)
             nc.vector.tensor_copy(
                 out=wg[:].bitcast(F32), in_=wt[:].rearrange("p a u n -> p a n u")
@@ -154,43 +165,37 @@ def tile_retentionmechanism_pa_t_kernel(tc, y, w_swiglu, out):
                 in_=wg[:].rearrange("p a n t -> p (a n t)"),
             )
 
-        for s in range(PAIRS + 2):
-            a = 2 * s
-            b = a + 1
-            if s < PAIRS:
-                transposes(a)
-                if s == 0:
+        waiting = []
+
+        def quantise_last(next_one):
+            for quantise, g in waiting:
+                quantise(g)
+            waiting.clear()
+            waiting.extend(next_one)
+
+        runs = [range(0, FIRST_RUN)]
+        for g in range(FIRST_RUN, GROUPS, RUN):
+            runs.append(range(g, min(g + RUN, GROUPS)))
+        before = range(0)
+        for run in runs + [range(0)]:
+            for g in run:
+                transposes(g)
+                if g == 0:
                     prepare_w()
-                transposes(b)
-            if 1 <= s <= PAIRS:
-                mm1(a - 2)
-                mm1(b - 2)
-            if s < PAIRS:
-                drain_y(a, 0)
-                drain_y(a, 1)
-            if s == PAIRS - 1:
-                for g in range(16):
-                    mm2(g)
-            if s >= 2:
-                quant_uv(b - 4)
-            if s < PAIRS:
-                drain_y(b, 0)
-                drain_y(b, 1)
-                quant_y(a)
-            if 1 <= s <= PAIRS:
-                drain_uv(a - 2, 0)
-                drain_uv(a - 2, 1)
-            if s < PAIRS:
-                quant_y(b)
-            if 1 <= s <= PAIRS:
-                drain_uv(b - 2, 0)
-                drain_uv(b - 2, 1)
-                quant_uv(a - 2)
-            if s == PAIRS:
-                for g in range(16, GROUPS - 2):
-                    mm2(g)
-        mm2(GROUPS - 2)
-        mm2(GROUPS - 1)
+                drain_y(g, 0)
+                drain_y(g, 1)
+                quantise_last([(quant_y, g)])
+            for g in before:
+                mm1(g)
+                drain_uv(g, 0)
+                drain_uv(g, 1)
+                quantise_last([(quant_uv, g)])
+            if len(before) == 0:
+                quantise_last([])
+            before = run
+        quantise_last([])
+        for g in range(GROUPS):
+            mm2(g)
 
         res = keep.tile([P, E], F32, name="res")
         nc.scalar.mul(res[:], acc[0][:], SCALE)

@@ -21,10 +21,10 @@ SCALE = 1.0 / 4.0 / (128.0 ** 0.5)
 
 FLOPS = 2 * TOKENS * FEATURES * 2 * E + 2 * TOKENS * E * E
 
-BANKS = 8
-FIRST_RUN = 2
+BANKS = 7
 RUN = 3
 DEPTH = 6
+WARM_UPS = 3
 
 
 def tile_retentionmechanism_pa_t_kernel(tc, y, w_swiglu, out):
@@ -41,9 +41,9 @@ def tile_retentionmechanism_pa_t_kernel(tc, y, w_swiglu, out):
         for g in range(GROUPS):
             y_sb.append(keep.tile([P, PACK, FEATURES], BF16, name="y%d" % g))
         w_sb = keep.tile([P, 2, FEATURES], BF16, name="w_sb")
-        nc.sync.dma_start(out=y_sb[0][:, 0:2, :], in_=y_rows[0][:, 0:2, :])
-        nc.scalar.dma_start(out=w_sb[:], in_=w_swiglu.rearrange("(a p) q -> p a q", p=P))
-        nc.sync.dma_start(out=y_sb[0][:, 2:4, :], in_=y_rows[0][:, 2:4, :])
+        for j in range(PACK):
+            nc.sync.dma_start(out=y_sb[0][:, j, :], in_=y_rows[0][:, j, :])
+        nc.sync.dma_start(out=w_sb[:], in_=w_swiglu.rearrange("(a p) q -> p a q", p=P))
         for g in range(1, GROUPS):
             nc.sync.dma_start(out=y_sb[g][:], in_=y_rows[g])
 
@@ -76,6 +76,14 @@ def tile_retentionmechanism_pa_t_kernel(tc, y, w_swiglu, out):
                     nc.tensor.transpose(xt[:, a, u, :], words[:, u * P:(u + 1) * P], ident[:])
             return xt
 
+        warm = keep.tile([P, 512], BF16, name="warm")
+        nc.vector.memset(warm[:], 0.0)
+        warm_bank = psum.tile([P, 512], F32, name="warm_bank", tag=next_bank())
+        for i in range(WARM_UPS):
+            nc.tensor.matmul(
+                warm_bank[:], lhsT=warm[:, 0:P], rhs=warm[:], start=True, stop=True
+            )
+
         xts = {}
         ygs = {}
         ycs = {}
@@ -92,7 +100,7 @@ def tile_retentionmechanism_pa_t_kernel(tc, y, w_swiglu, out):
                     [P, PACK, P, PACK], BF16, name="yg", tag="yg%d" % (g % DEPTH), align_bytes=64
                 )
             dst = ygs[g][:].bitcast(F32)[:, 2 * h:2 * h + 2, :, :]
-            drain(dst, xts[(g, h)][:].rearrange("p a u n -> p a n u"), (2 * g + h) % 4 == 3)
+            drain(dst, xts[(g, h)][:].rearrange("p a u n -> p a n u"), (2 * g + h) % 16 % 3 == 2)
 
         def quant_y(g):
             codes = ring.tile([P, GROUP], U32, name="yc", tag="yc%d" % (g % DEPTH), align_bytes=64)
@@ -128,7 +136,7 @@ def tile_retentionmechanism_pa_t_kernel(tc, y, w_swiglu, out):
             drain(
                 ugs[g][:, h, :, :],
                 uvs[(g, h)][:].rearrange("p j d -> p d j"),
-                (2 * g + h) % 16 in range(3, 16, 3),
+                (2 * g + h) % 4 == 0,
             )
 
         def quant_uv(g):
@@ -142,7 +150,7 @@ def tile_retentionmechanism_pa_t_kernel(tc, y, w_swiglu, out):
 
         def mm2(g):
             if g == 0:
-                acc.append(psum.tile([P, E], F32, name="acc", tag=next_bank()))
+                acc.append(psum.tile([P, E], F32, name="acc", tag="bank7"))
             nc.tensor.matmul_mx(
                 out=acc[0][:],
                 lhsT=uv_codes[:, g, 0:E].bitcast(FP8X4),
@@ -153,12 +161,15 @@ def tile_retentionmechanism_pa_t_kernel(tc, y, w_swiglu, out):
                 stop=(g == GROUPS - 1),
             )
 
-        def prepare_w():
-            wt = transpose_two(w_sb[:, 0, :], w_sb[:, 1, :])
-            wg = keep.tile([P, 2, E, PACK], BF16, name="wg", align_bytes=64)
-            nc.vector.tensor_copy(
-                out=wg[:].bitcast(F32), in_=wt[:].rearrange("p a u n -> p a n u")
-            )
+        wg = keep.tile([P, 2, E, PACK], BF16, name="wg", align_bytes=64)
+
+        def transpose_w():
+            return transpose_two(w_sb[:, 0, :], w_sb[:, 1, :])
+
+        def drain_w(wt):
+            nc.scalar.copy(out=wg[:].bitcast(F32), in_=wt[:].rearrange("p a u n -> p a n u"))
+
+        def quant_w():
             nc.vector.quantize_mx(
                 out=w_codes[:].bitcast(FP8X4),
                 scales=w_scales[:],
@@ -173,28 +184,39 @@ def tile_retentionmechanism_pa_t_kernel(tc, y, w_swiglu, out):
             waiting.clear()
             waiting.extend(next_one)
 
-        runs = [range(0, FIRST_RUN)]
-        for g in range(FIRST_RUN, GROUPS, RUN):
-            runs.append(range(g, min(g + RUN, GROUPS)))
+        runs = [range(0, 1)]
+        for g in range(1, GROUPS):
+            if len(runs) > 2 and len(runs[-1]) < RUN:
+                runs[-1] = range(runs[-1][0], g + 1)
+            else:
+                runs.append(range(g, g + 1))
         before = range(0)
+        quantised = range(0)
         for run in runs + [range(0)]:
             for g in run:
                 transposes(g)
                 if g == 0:
-                    prepare_w()
+                    wt = transpose_w()
                 drain_y(g, 0)
                 drain_y(g, 1)
                 quantise_last([(quant_y, g)])
+                if g == 0:
+                    drain_w(wt)
+                    quantise_last([])
+                    quant_w()
             for g in before:
                 mm1(g)
                 drain_uv(g, 0)
                 drain_uv(g, 1)
                 quantise_last([(quant_uv, g)])
+            for g in quantised:
+                mm2(g)
             if len(before) == 0:
                 quantise_last([])
+            quantised = before
             before = run
         quantise_last([])
-        for g in range(GROUPS):
+        for g in quantised:
             mm2(g)
 
         res = keep.tile([P, E], F32, name="res")

@@ -22,7 +22,7 @@ SCALE = 1.0 / 4.0 / (128.0 ** 0.5)
 FLOPS = 2 * TOKENS * FEATURES * 2 * E + 2 * TOKENS * E * E
 
 BANKS = 7
-RUN = 3
+RUN = 2
 DEPTH = 6
 WARM_UPS = 3
 
@@ -100,7 +100,7 @@ def tile_retentionmechanism_pa_t_kernel(tc, y, w_swiglu, out):
                     [P, PACK, P, PACK], BF16, name="yg", tag="yg%d" % (g % DEPTH), align_bytes=64
                 )
             dst = ygs[g][:].bitcast(F32)[:, 2 * h:2 * h + 2, :, :]
-            drain(dst, xts[(g, h)][:].rearrange("p a u n -> p a n u"), (2 * g + h) % 16 % 3 == 2)
+            drain(dst, xts[(g, h)][:].rearrange("p a u n -> p a n u"), (2 * g + h) % 16 in range(0, 15, 3))
 
         def quant_y(g):
             codes = ring.tile([P, GROUP], U32, name="yc", tag="yc%d" % (g % DEPTH), align_bytes=64)
@@ -136,7 +136,7 @@ def tile_retentionmechanism_pa_t_kernel(tc, y, w_swiglu, out):
             drain(
                 ugs[g][:, h, :, :],
                 uvs[(g, h)][:].rearrange("p j d -> p d j"),
-                (2 * g + h) % 4 == 0,
+                (2 * g + h) % 4 == 3,
             )
 
         def quant_uv(g):

from contextlib import ExitStack

import concourse.mybir as mybir
from concourse.masks import make_identity

F32 = mybir.dt.float32
BF16 = mybir.dt.bfloat16
U32 = mybir.dt.uint32
U8 = mybir.dt.uint8
FP8X4 = mybir.dt.float8_e4m3fn_x4

P = 128
PACK = 4
TOKENS = 4 * 4096
FEATURES = 512
E = 128
GROUP = P * PACK
GROUPS = TOKENS // GROUP
WORDS = FEATURES // 2
SCALE = 1.0 / 4.0 / (128.0 ** 0.5)

FLOPS = 2 * TOKENS * FEATURES * 2 * E + 2 * TOKENS * E * E

BANKS = 7
RUN = 2
DEPTH = 6
WARM_UPS = 3


def tile_retentionmechanism_pa_t_kernel(tc, y, w_swiglu, out):
    nc = tc.nc
    with ExitStack() as ctx:
        ctx.enter_context(tc.manual_schedule())
        keep = ctx.enter_context(tc.tile_pool(name="keep", bufs=1))
        ring = ctx.enter_context(tc.tile_pool(name="ring", bufs=1))
        psum = ctx.enter_context(tc.psum_pool(name="psum", bufs=1))

        y_rows = y.flatten_outer_dims().rearrange("(g p j) q -> g p j q", p=P, j=PACK)

        y_sb = []
        for g in range(GROUPS):
            y_sb.append(keep.tile([P, PACK, FEATURES], BF16, name="y%d" % g))
        w_sb = keep.tile([P, 2, FEATURES], BF16, name="w_sb")
        for j in range(PACK):
            nc.sync.dma_start(out=y_sb[0][:, j, :], in_=y_rows[0][:, j, :])
        nc.sync.dma_start(out=w_sb[:], in_=w_swiglu.rearrange("(a p) q -> p a q", p=P))
        for g in range(1, GROUPS):
            nc.sync.dma_start(out=y_sb[g][:], in_=y_rows[g])

        ident = keep.tile([P, P], F32, name="ident")
        make_identity(nc, ident[:])

        w_codes = keep.tile([P, 2 * E], U32, name="w_codes", align_bytes=64)
        w_scales = keep.tile([P, 2 * E], U8, name="w_scales", align_bytes=64)
        uv_codes = keep.tile([P, GROUPS, 2 * E], U32, name="uv_codes", align_bytes=64)
        uv_scales = keep.tile([P, GROUPS, 2 * E], U8, name="uv_scales", align_bytes=64)

        state = {"fills": 0}

        def next_bank():
            fills = state["fills"]
            state["fills"] = fills + 1
            return "bank%d" % (fills % BANKS)

        def drain(dst, src, on_vector):
            if on_vector:
                nc.vector.tensor_copy(out=dst, in_=src)
            else:
                nc.scalar.copy(out=dst, in_=src)

        def transpose_two(rows_a, rows_b):
            xt = psum.tile([P, 2, 2, P], F32, name="xt", tag=next_bank())
            for a, rows in enumerate((rows_a, rows_b)):
                words = rows.bitcast(F32)
                for u in range(2):
                    nc.tensor.transpose(xt[:, a, u, :], words[:, u * P:(u + 1) * P], ident[:])
            return xt

        warm = keep.tile([P, 512], BF16, name="warm")
        nc.vector.memset(warm[:], 0.0)
        warm_bank = psum.tile([P, 512], F32, name="warm_bank", tag=next_bank())
        for i in range(WARM_UPS):
            nc.tensor.matmul(
                warm_bank[:], lhsT=warm[:, 0:P], rhs=warm[:], start=True, stop=True
            )

        xts = {}
        ygs = {}
        ycs = {}
        uvs = {}
        ugs = {}

        def transposes(g):
            for h in range(2):
                xts[(g, h)] = transpose_two(y_sb[g][:, 2 * h, :], y_sb[g][:, 2 * h + 1, :])

        def drain_y(g, h):
            if h == 0:
                ygs[g] = ring.tile(
                    [P, PACK, P, PACK], BF16, name="yg", tag="yg%d" % (g % DEPTH), align_bytes=64
                )
            dst = ygs[g][:].bitcast(F32)[:, 2 * h:2 * h + 2, :, :]
            drain(dst, xts[(g, h)][:].rearrange("p a u n -> p a n u"), (2 * g + h) % 16 in range(0, 15, 3))

        def quant_y(g):
            codes = ring.tile([P, GROUP], U32, name="yc", tag="yc%d" % (g % DEPTH), align_bytes=64)
            scales = ring.tile([P, GROUP], U8, name="ys", tag="ys%d" % (g % DEPTH), align_bytes=64)
            nc.vector.quantize_mx(
                out=codes[:].bitcast(FP8X4),
                scales=scales[:],
                in_=ygs[g][:].rearrange("p j n t -> p (j n t)"),
            )
            ycs[g] = (codes, scales)

        def mm1(g):
            codes, scales = ycs[g]
            for h in range(2):
                bank = psum.tile([P, PACK, E], F32, name="uv", tag=next_bank())
                for j in range(PACK):
                    nc.tensor.matmul_mx(
                        out=bank[:, j, :],
                        lhsT=codes[:, j * P:(j + 1) * P].bitcast(FP8X4),
                        lhsT_scale=scales[:, j * P:(j + 1) * P],
                        rhs=w_codes[:, h * E:(h + 1) * E].bitcast(FP8X4),
                        rhs_scale=w_scales[:, h * E:(h + 1) * E],
                        start=True,
                        stop=True,
                    )
                uvs[(g, h)] = bank

        def drain_uv(g, h):
            if h == 0:
                ugs[g] = ring.tile(
                    [P, 2, E, PACK], BF16, name="ug", tag="ug%d" % (g % DEPTH), align_bytes=64
                )
            drain(
                ugs[g][:, h, :, :],
                uvs[(g, h)][:].rearrange("p j d -> p d j"),
                (2 * g + h) % 4 == 3,
            )

        def quant_uv(g):
            nc.vector.quantize_mx(
                out=uv_codes[:, g, :].bitcast(FP8X4),
                scales=uv_scales[:, g, :],
                in_=ugs[g][:].rearrange("p h d j -> p (h d j)"),
            )

        acc = []

        def mm2(g):
            if g == 0:
                acc.append(psum.tile([P, E], F32, name="acc", tag="bank7"))
            nc.tensor.matmul_mx(
                out=acc[0][:],
                lhsT=uv_codes[:, g, 0:E].bitcast(FP8X4),
                lhsT_scale=uv_scales[:, g, 0:E],
                rhs=uv_codes[:, g, E:2 * E].bitcast(FP8X4),
                rhs_scale=uv_scales[:, g, E:2 * E],
                start=(g == 0),
                stop=(g == GROUPS - 1),
            )

        wg = keep.tile([P, 2, E, PACK], BF16, name="wg", align_bytes=64)

        def transpose_w():
            return transpose_two(w_sb[:, 0, :], w_sb[:, 1, :])

        def drain_w(wt):
            nc.scalar.copy(out=wg[:].bitcast(F32), in_=wt[:].rearrange("p a u n -> p a n u"))

        def quant_w():
            nc.vector.quantize_mx(
                out=w_codes[:].bitcast(FP8X4),
                scales=w_scales[:],
                in_=wg[:].rearrange("p a n t -> p (a n t)"),
            )

        waiting = []

        def quantise_last(next_one):
            for quantise, g in waiting:
                quantise(g)
            waiting.clear()
            waiting.extend(next_one)

        runs = [range(0, 1)]
        for g in range(1, GROUPS):
            if len(runs) > 2 and len(runs[-1]) < RUN:
                runs[-1] = range(runs[-1][0], g + 1)
            else:
                runs.append(range(g, g + 1))
        before = range(0)
        quantised = range(0)
        for run in runs + [range(0)]:
            for g in run:
                transposes(g)
                if g == 0:
                    wt = transpose_w()
                drain_y(g, 0)
                drain_y(g, 1)
                quantise_last([(quant_y, g)])
                if g == 0:
                    drain_w(wt)
                    quantise_last([])
                    quant_w()
            for g in before:
                mm1(g)
                drain_uv(g, 0)
                drain_uv(g, 1)
                quantise_last([(quant_uv, g)])
            for g in quantised:
                mm2(g)
            if len(before) == 0:
                quantise_last([])
            quantised = before
            before = run
        quantise_last([])
        for g in quantised:
            mm2(g)

        res = keep.tile([P, E], F32, name="res")
        nc.scalar.mul(res[:], acc[0][:], SCALE)
        nc.sync.dma_start(out=out, in_=res[:])
